import numpy as np
import ml_dtypes


def mxq(x, axis, fmt="e4m3"):
    dtype, down = {"e4m3": (ml_dtypes.float8_e4m3fn, 7), "e5m2": (ml_dtypes.float8_e5m2, 14)}[fmt]
    v = np.moveaxis(np.asarray(x, np.float32).astype(ml_dtypes.bfloat16).astype(np.float64), axis, -1)
    blocks = v.reshape(v.shape[:-1] + (-1, 32))
    amax = np.abs(blocks).max(-1, keepdims=True)
    byte = np.maximum(np.where(amax > 0, np.frexp(amax)[1] - 1 + 127, 0) - down, 1)
    scale = np.exp2(byte - 127.0)
    codes = (blocks / scale).astype(np.float32).astype(dtype).astype(np.float64)
    return np.moveaxis((codes * scale).reshape(v.shape), -1, axis)


WIDE = False


def mx_kscale(k):
    if not WIDE:
        return np.ones(k)
    levels = np.array([10, -10, 5, -5, 0])
    if k % 512:
        return np.exp2(np.random.permutation(np.resize(levels, k // 32))).repeat(32)
    a = np.empty((k // 512, 16))
    for p in range(k // 512):
        a[p, :8] = np.random.permutation(np.resize(levels, 8))
        for g in range(8):
            far = levels[np.abs(levels - a[p, g]) >= 10]
            a[p, g + 8] = far[np.random.randint(len(far))]
    return np.exp2(a.ravel()).repeat(32)


BF16 = ml_dtypes.bfloat16


def bf(x):
    return np.asarray(x, np.float32).astype(BF16)


def f64(x):
    return np.asarray(x).astype(np.float64)


B, S, D, F, F2 = 4, 256, 512, 2048, 1024
EPS = 1e-6
D2 = 2 * D


def setup_inputs():
    n = np.random.standard_normal
    s, t = mx_kscale(F), mx_kscale(D2)
    tr, ti = t[:D], t[D:]
    wd = 1.5 / np.sqrt(F)
    return {'h_r': bf(n((B, S, F)) * 0.6 * s), 'h_i': bf(n((B, S, F)) * 0.6 * s),
            'w2r': bf(n((F, D)) * wd / s[:, None] * tr), 'b2r': bf(n(D) * 0.2 * tr),
            'w2i': bf(n((F, D)) * wd / s[:, None] * ti), 'b2i': bf(n(D) * 0.2 * ti),
            'We': bf(n((D2, D)) / np.sqrt(D2) / t[:, None]), 'be': bf(n(D) * 0.2),
            'g_rms': bf(1.0 + 0.1 * n(D))}


def reference(h_r, h_i, w2r, b2r, w2i, b2i, We, be, g_rms):
    rp = (mxq(f64(h_r), 2, 'e4m3') @ mxq(f64(w2r), 0, 'e4m3')) + f64(b2r)
    ip = (mxq(f64(h_i), 2, 'e4m3') @ mxq(f64(w2i), 0, 'e4m3')) + f64(b2i)
    cat = np.concatenate([rp, ip], axis=-1)
    wave = (mxq(cat, 2, 'e4m3') @ mxq(f64(We), 0, 'e4m3')) + f64(be)
    return wave * (1.0 / np.sqrt(np.mean(wave * wave, axis=-1, keepdims=True) + EPS)) * f64(g_rms)

@@ -1,0 +1,316 @@
+from contextlib import ExitStack
+
+import concourse.mybir as mybir
+from concourse.masks import make_identity
+
+F32 = mybir.dt.float32
+BF16 = mybir.dt.bfloat16
+U32 = mybir.dt.uint32
+U8 = mybir.dt.uint8
+FP8X4 = mybir.dt.float8_e4m3fn_x4
+ACT = mybir.ActivationFunctionType
+ALU = mybir.AluOpType
+
+P = 128
+PACK = 4
+K_PASS = P * PACK
+TOKENS = 1024
+F = 2048
+D = 512
+EPS = 1e-6
+
+STREAMS = 2
+PASSES = F // K_PASS
+D_TILES = D // P
+TOKEN_TILES = TOKENS // P
+TILES = 2
+QUARTERS = TOKEN_TILES // TILES
+COLS = TILES * P
+WORDS = F // 2
+BANKS = 8
+FIRST_STEP = -1
+
+FLOPS = 2 * TOKENS * F * D * STREAMS + 2 * TOKENS * (STREAMS * D) * D
+
+
+def regroup(nc, grouped, rows):
+    src = rows.rearrange("p (t c i) -> p c t i", t=PACK, i=4)
+    dst = grouped.rearrange("p (c i t) -> p c t i", i=4, t=PACK)
+    nc.vector.tensor_copy(out=dst, in_=src)
+
+
+def regroup_by_channel(nc, grouped, rows):
+    src = rows.rearrange("p (j m t) -> p t m j", j=PACK, t=PACK)
+    dst = grouped.rearrange("p (t m j) -> p t m j", t=PACK, j=PACK)
+    nc.vector.tensor_copy(out=dst, in_=src)
+
+
+def tile_wavenetworklm_pb_kernel(tc, h_r, h_i, w2r, b2r, w2i, b2i, We, be, g_rms, out):
+    nc = tc.nc
+    hidden = (h_r, h_i)
+    weights = (w2r, w2i)
+    biases = (b2r, b2i)
+    units = [(s, q) for s in range(STREAMS) for q in range(QUARTERS)]
+
+    with ExitStack() as ctx:
+        ctx.enter_context(tc.manual_schedule())
+        const = ctx.enter_context(tc.tile_pool(name="const", bufs=1))
+        raw = ctx.enter_context(tc.tile_pool(name="raw", bufs=1))
+        keep = ctx.enter_context(tc.tile_pool(name="keep", bufs=1))
+        stage = ctx.enter_context(tc.tile_pool(name="stage", bufs=2))
+        tail = ctx.enter_context(tc.tile_pool(name="tail", bufs=3))
+        acc_pool = ctx.enter_context(tc.psum_pool(name="acc", bufs=1))
+        work_pool = ctx.enter_context(tc.psum_pool(name="work", bufs=BANKS - D_TILES))
+
+        first_chunks = [(0, g) for g in range(PASSES)]
+        later_chunks = [(1, g) for g in range(PASSES)] + [(2, g) for g in range(STREAMS)]
+
+        def chunks_of_step(step):
+            if step == FIRST_STEP:
+                return first_chunks
+            if step == 0:
+                return later_chunks[0:2]
+            return later_chunks[step + 1 : step + 2]
+
+        h_raw = {}
+        w_raw = {}
+
+        def load_hidden(s, q):
+            view = hidden[s].flatten_outer_dims().rearrange("(p j) k -> p (j k)", j=TOKEN_TILES)
+            rows = raw.tile([P, TILES * F], BF16, name="h_raw_%d_%d" % (s, q))
+            nc.sync.dma_start(out=rows[:], in_=view[:, TILES * F * q : TILES * F * (q + 1)])
+            h_raw[(s, q)] = rows
+
+        def load_chunk(matrix, g):
+            rows = raw.tile([P, PACK * D], BF16, name="w_raw_%d_%d" % (matrix, g))
+            source = (w2r, w2i, We)[matrix]
+            view = source.rearrange("(c p t) n -> c p (t n)", p=P, t=PACK)
+            nc.sync.dma_start(out=rows[:], in_=view[g])
+            w_raw[(matrix, g)] = rows
+
+        for step in range(FIRST_STEP, len(units) - 1):
+            load_hidden(*units[step + 1])
+            for chunk in chunks_of_step(step):
+                load_chunk(*chunk)
+
+        row_zero = const.tile([P, 2 * D], BF16)
+        nc.vector.memset(row_zero[:], 0.0)
+        bias_raw = [const.tile([P, PACK], BF16, name="bias_raw_%d" % s) for s in range(STREAMS)]
+        for s in range(STREAMS):
+            nc.scalar.dma_start(out=bias_raw[s][:], in_=biases[s].rearrange("(p t) -> p t", t=PACK))
+        nc.scalar.dma_start(out=row_zero[0:1, 0:D], in_=be.rearrange("(o n) -> o n", o=1))
+        nc.scalar.dma_start(out=row_zero[0:1, D : 2 * D], in_=g_rms.rearrange("(o n) -> o n", o=1))
+
+        eps = const.tile([P, 1], F32)
+        nc.vector.memset(eps[:], EPS)
+        warm = const.tile([P, 1], F32)
+        nc.scalar.activation(out=warm[:], in_=eps[:], func=ACT.Sqrt)
+        ident_f32 = const.tile([P, P], F32)
+        make_identity(nc, ident_f32[:])
+        ones = const.tile([P, P], BF16)
+        nc.vector.memset(ones[:], 1.0)
+        b2 = const.tile([P, STREAMS * D_TILES], F32)
+        be_all = const.tile([P, D], F32)
+        g_all = const.tile([P, D], F32)
+
+        def spread_small_vectors():
+            for s in range(STREAMS):
+                nc.vector.tensor_copy(out=b2[:, PACK * s : PACK * (s + 1)], in_=bias_raw[s][:])
+            for i, dest in enumerate((be_all, g_all)):
+                spread = work_pool.tile([P, D], F32, tag="work")
+                nc.tensor.matmul(
+                    spread[:], lhsT=ones[:], rhs=row_zero[:, D * i : D * (i + 1)], start=True, stop=True
+                )
+                nc.scalar.copy(out=dest[:], in_=spread[:])
+
+        chunks_in = (PASSES, PASSES, STREAMS)
+        w_codes = [keep.tile([P, n, D], U32, align_bytes=64, name="w_codes_%d" % i) for i, n in enumerate(chunks_in)]
+        w_scales = [keep.tile([P, n, D], U8, align_bytes=64, name="w_scales_%d" % i) for i, n in enumerate(chunks_in)]
+        w_grouped = {}
+        h_grouped = {}
+        h_codes = {}
+        h_scales = {}
+        acc = {}
+        cat_plain = {}
+        cat_grouped = {}
+        cat_codes = {}
+        cat_scales = {}
+        y_banks = {}
+        waves = {}
+        totals = {}
+        roots = {}
+        inverses = {}
+
+        def regroup_chunk(matrix, g):
+            grouped = stage.tile([P, PACK * D], BF16, align_bytes=64, tag="w_grouped", bufs=3)
+            if matrix < STREAMS:
+                regroup_by_channel(nc, grouped[:], w_raw[(matrix, g)][:])
+            else:
+                regroup(nc, grouped[:], w_raw[(matrix, g)][:])
+            w_grouped[(matrix, g)] = grouped
+
+        def quantise_chunk(matrix, g):
+            nc.vector.quantize_mx(
+                out=w_codes[matrix][:, g, :].bitcast(FP8X4),
+                scales=w_scales[matrix][:, g, :],
+                in_=w_grouped[(matrix, g)][:],
+            )
+
+        def flip_hidden(s, q):
+            words = h_raw[(s, q)][:].bitcast(F32)
+            grouped = stage.tile([P, PASSES * PACK * COLS], BF16, align_bytes=64, tag="h_grouped")
+            pairs = grouped[:].bitcast(F32).rearrange("p (g j r u) -> p g j r u", g=PASSES, j=TILES, u=2)
+            for g in range(PASSES):
+                flipped = work_pool.tile([P, TILES * 2, P], F32, tag="work")
+                for j in range(TILES):
+                    for u in range(2):
+                        first = j * WORDS + g * (K_PASS // 2)
+                        nc.tensor.transpose(
+                            flipped[:, 2 * j + u, :], words[:, first + u : first + K_PASS // 2 : 2], ident_f32[:]
+                        )
+                nc.scalar.copy(out=pairs[:, g], in_=flipped[:].rearrange("p (j u) r -> p j r u", u=2))
+            h_grouped[(s, q)] = grouped
+
+        def quantise_hidden(s, q):
+            codes = stage.tile([P, PASSES * COLS], U32, align_bytes=64, tag="h_codes")
+            scales = stage.tile([P, PASSES * COLS], U8, align_bytes=64, tag="h_scales")
+            nc.vector.quantize_mx(out=codes[:].bitcast(FP8X4), scales=scales[:], in_=h_grouped[(s, q)][:])
+            h_codes[(s, q)] = codes
+            h_scales[(s, q)] = scales
+
+        def first_stage(s, q):
+            for m in range(D_TILES):
+                acc[m] = acc_pool.tile([P, COLS], F32, name="acc_%d" % m)
+                rows = slice(P * m, P * (m + 1))
+                for g in range(PASSES):
+                    cols = slice(COLS * g, COLS * (g + 1))
+                    nc.tensor.matmul_mx(
+                        out=acc[m][:],
+                        lhsT=w_codes[s][:, g, rows].bitcast(FP8X4),
+                        lhsT_scale=w_scales[s][:, g, rows],
+                        rhs=h_codes[(s, q)][:, cols].bitcast(FP8X4),
+                        rhs_scale=h_scales[(s, q)][:, cols],
+                        start=(g == 0),
+                        stop=(g == PASSES - 1),
+                    )
+
+        def add_first_bias(s, q):
+            plain = stage.tile([P, D_TILES * COLS], BF16, tag="cat_plain")
+            for m in range(D_TILES):
+                nc.scalar.activation(
+                    out=plain[:, COLS * m : COLS * (m + 1)],
+                    in_=acc[m][:],
+                    func=ACT.Identity,
+                    bias=b2[:, D_TILES * s + m : D_TILES * s + m + 1],
+                    scale=1.0,
+                )
+            cat_plain[(s, q)] = plain
+
+        def regroup_cat(s, q):
+            grouped = stage.tile([P, PACK * COLS], BF16, align_bytes=64, tag="cat_grouped")
+            regroup(nc, grouped[:], cat_plain[(s, q)][:])
+            cat_grouped[(s, q)] = grouped
+
+        def quantise_cat(s, q):
+            codes = keep.tile([P, COLS], U32, align_bytes=64, name="cat_codes_%d_%d" % (s, q))
+            scales = keep.tile([P, COLS], U8, align_bytes=64, name="cat_scales_%d_%d" % (s, q))
+            nc.vector.quantize_mx(out=codes[:].bitcast(FP8X4), scales=scales[:], in_=cat_grouped[(s, q)][:])
+            cat_codes[(s, q)] = codes
+            cat_scales[(s, q)] = scales
+
+        def second_stage(q):
+            for j in range(TILES):
+                cols = slice(P * j, P * (j + 1))
+                y = work_pool.tile([P, D], F32, tag="work")
+                for s in range(STREAMS):
+                    nc.tensor.matmul_mx(
+                        out=y[:],
+                        lhsT=cat_codes[(s, q)][:, cols].bitcast(FP8X4),
+                        lhsT_scale=cat_scales[(s, q)][:, cols],
+                        rhs=w_codes[2][:, s, :].bitcast(FP8X4),
+                        rhs_scale=w_scales[2][:, s, :],
+                        start=(s == 0),
+                        stop=(s == STREAMS - 1),
+                    )
+                y_banks[(q, j)] = y
+
+        def add_second_bias(q):
+            for j in range(TILES):
+                wave = tail.tile([P, D], F32, tag="wave", bufs=3 * TILES)
+                nc.vector.tensor_tensor(out=wave[:], in0=y_banks[(q, j)][:], in1=be_all[:], op=ALU.add)
+                waves[(q, j)] = wave
+
+        def sum_squares(q):
+            total = tail.tile([P, TILES], F32, tag="total")
+            for j in range(TILES):
+                squares = tail.tile([P, D], BF16, tag="squares")
+                nc.scalar.activation(
+                    out=squares[:], in_=waves[(q, j)][:], func=ACT.Square, accum_out=total[:, j : j + 1]
+                )
+            totals[q] = total
+
+        def root_mean_square(q):
+            rms = tail.tile([P, TILES], F32, tag="rms")
+            nc.scalar.activation(out=rms[:], in_=totals[q][:], func=ACT.Sqrt, bias=eps[:], scale=1.0 / D)
+            roots[q] = rms
+
+        def invert_rms(q):
+            inv = tail.tile([P, TILES], F32, tag="inv")
+            nc.vector.reciprocal(out=inv[:], in_=roots[q][:])
+            inverses[q] = inv
+
+        out_view = out.flatten_outer_dims().rearrange("(p j) d -> p j d", j=TOKEN_TILES)
+
+        def normalise_tile(q, j):
+            normed = tail.tile([P, D], F32, tag="normed", bufs=2 * TILES)
+            nc.vector.scalar_tensor_tensor(
+                out=normed[:],
+                in0=waves[(q, j)][:],
+                scalar=inverses[q][:, j : j + 1],
+                in1=g_all[:],
+                op0=ALU.mult,
+                op1=ALU.mult,
+            )
+            nc.sync.dma_start(out=out_view[:, TILES * q + j, :], in_=normed[:])
+
+        def unit_at(i):
+            return [units[i]] if 0 <= i < len(units) else []
+
+        def quarter_at(i):
+            return [q for s, q in unit_at(i) if s == STREAMS - 1]
+
+        for step in range(FIRST_STEP, len(units) + 3):
+            chunks = chunks_of_step(step)
+            for q in quarter_at(step - 2):
+                add_second_bias(q)
+            for s, q in unit_at(step + 1):
+                flip_hidden(s, q)
+            for q in quarter_at(step - 3):
+                invert_rms(q)
+            for s, q in unit_at(step - 1):
+                regroup_cat(s, q)
+            for i, chunk in enumerate(chunks):
+                regroup_chunk(*chunk)
+                if i > 0:
+                    quantise_chunk(*chunks[i - 1])
+            for q in quarter_at(step - 3):
+                normalise_tile(q, 0)
+            for s, q in unit_at(step - 1):
+                quantise_cat(s, q)
+            for q in quarter_at(step - 3):
+                normalise_tile(q, 1)
+            for chunk in chunks[-1:]:
+                quantise_chunk(*chunk)
+            if step == FIRST_STEP:
+                spread_small_vectors()
+            for q in quarter_at(step - 2):
+                sum_squares(q)
+            for s, q in unit_at(step):
+                first_stage(s, q)
+                add_first_bias(s, q)
+            for q in quarter_at(step - 1):
+                second_stage(q)
+            for q in quarter_at(step - 2):
+                root_mean_square(q)
+            for s, q in unit_at(step + 1):
+                quantise_hidden(s, q)

@@ -40,8 +40,8 @@ def regroup(nc, grouped, rows):
 
 
 def regroup_by_channel(nc, grouped, rows):
-    src = rows.rearrange("p (j m t) -> p t m j", j=PACK, t=PACK)
-    dst = grouped.rearrange("p (t m j) -> p t m j", t=PACK, j=PACK)
+    src = rows.rearrange("p (j m t) -> p m j t", j=PACK, t=PACK)
+    dst = grouped.rearrange("p (t m j) -> p m j t", t=PACK, j=PACK)
     nc.vector.tensor_copy(out=dst, in_=src)
 
 

@@ -26,9 +26,8 @@ TOKEN_TILES = TOKENS // P
 TILES = 2
 QUARTERS = TOKEN_TILES // TILES
 COLS = TILES * P
-WORDS = F // 2
-BANKS = 8
-FIRST_STEP = -1
+PAIR_PASSES = 2
+LOOKAHEAD = 2
 
 FLOPS = 2 * TOKENS * F * D * STREAMS + 2 * TOKENS * (STREAMS * D) * D
 
@@ -48,7 +47,7 @@ def regroup_by_channel(nc, grouped, rows):
 def tile_wavenetworklm_pb_kernel(tc, h_r, h_i, w2r, b2r, w2i, b2i, We, be, g_rms, out):
     nc = tc.nc
     hidden = (h_r, h_i)
-    weights = (w2r, w2i)
+    matrices = (w2r, w2i, We)
     biases = (b2r, b2i)
     units = [(s, q) for s in range(STREAMS) for q in range(QUARTERS)]
 
@@ -59,45 +58,51 @@ def tile_wavenetworklm_pb_kernel(tc, h_r, h_i, w2r, b2r, w2i, b2i, We, be, g_rms
         keep = ctx.enter_context(tc.tile_pool(name="keep", bufs=1))
         stage = ctx.enter_context(tc.tile_pool(name="stage", bufs=2))
         tail = ctx.enter_context(tc.tile_pool(name="tail", bufs=3))
-        acc_pool = ctx.enter_context(tc.psum_pool(name="acc", bufs=1))
-        work_pool = ctx.enter_context(tc.psum_pool(name="work", bufs=BANKS - D_TILES))
-
-        first_chunks = [(0, g) for g in range(PASSES)]
-        later_chunks = [(1, g) for g in range(PASSES)] + [(2, g) for g in range(STREAMS)]
-
-        def chunks_of_step(step):
-            if step == FIRST_STEP:
-                return first_chunks
-            if step == 0:
-                return later_chunks[0:2]
-            return later_chunks[step + 1 : step + 2]
+        acc_pool = ctx.enter_context(tc.psum_pool(name="acc", bufs=3))
+        flip_pool = ctx.enter_context(tc.psum_pool(name="flip", bufs=3))
+        y_pool = ctx.enter_context(tc.psum_pool(name="y", bufs=2))
 
         h_raw = {}
         w_raw = {}
 
-        def load_hidden(s, q):
-            view = hidden[s].flatten_outer_dims().rearrange("(p j) k -> p (j k)", j=TOKEN_TILES)
-            rows = raw.tile([P, TILES * F], BF16, name="h_raw_%d_%d" % (s, q))
-            nc.sync.dma_start(out=rows[:], in_=view[:, TILES * F * q : TILES * F * (q + 1)])
-            h_raw[(s, q)] = rows
+        def load_hidden(s, tile):
+            view = hidden[s].flatten_outer_dims().rearrange("(p j) k -> j p k", j=TOKEN_TILES)
+            rows = raw.tile([P, F], BF16, name="h_raw_%d_%d" % (s, tile))
+            nc.sync.dma_start(out=rows[:], in_=view[tile])
+            h_raw[(s, tile)] = rows
 
         def load_chunk(matrix, g):
             rows = raw.tile([P, PACK * D], BF16, name="w_raw_%d_%d" % (matrix, g))
-            source = (w2r, w2i, We)[matrix]
-            view = source.rearrange("(c p t) n -> c p (t n)", p=P, t=PACK)
+            view = matrices[matrix].rearrange("(c p t) n -> c p (t n)", p=P, t=PACK)
             nc.sync.dma_start(out=rows[:], in_=view[g])
             w_raw[(matrix, g)] = rows
 
-        for step in range(FIRST_STEP, len(units) - 1):
-            load_hidden(*units[step + 1])
-            for chunk in chunks_of_step(step):
-                load_chunk(*chunk)
+        load_hidden(0, 0)
+        load_chunk(0, 0)
+        load_hidden(0, 1)
+        load_chunk(0, 1)
+        load_chunk(0, 2)
+        load_hidden(0, 2)
+        load_chunk(0, 3)
+        for tile in range(3, 6):
+            load_hidden(0, tile)
+        load_chunk(1, 0)
+        load_hidden(0, 6)
+        load_hidden(0, 7)
+        for g in range(1, PASSES):
+            load_chunk(1, g)
+        for tile in range(0, 4):
+            load_hidden(1, tile)
+        for g in range(STREAMS):
+            load_chunk(2, g)
+        for tile in range(4, TOKEN_TILES):
+            load_hidden(1, tile)
 
-        row_zero = const.tile([P, 2 * D], BF16)
-        nc.vector.memset(row_zero[:], 0.0)
         bias_raw = [const.tile([P, PACK], BF16, name="bias_raw_%d" % s) for s in range(STREAMS)]
         for s in range(STREAMS):
             nc.scalar.dma_start(out=bias_raw[s][:], in_=biases[s].rearrange("(p t) -> p t", t=PACK))
+        row_zero = const.tile([P, 2 * D], BF16)
+        nc.vector.memset(row_zero[:], 0.0)
         nc.scalar.dma_start(out=row_zero[0:1, 0:D], in_=be.rearrange("(o n) -> o n", o=1))
         nc.scalar.dma_start(out=row_zero[0:1, D : 2 * D], in_=g_rms.rearrange("(o n) -> o n", o=1))
 
@@ -113,11 +118,13 @@ def tile_wavenetworklm_pb_kernel(tc, h_r, h_i, w2r, b2r, w2i, b2i, We, be, g_rms
         be_all = const.tile([P, D], F32)
         g_all = const.tile([P, D], F32)
 
-        def spread_small_vectors():
+        def widen_first_bias():
             for s in range(STREAMS):
                 nc.vector.tensor_copy(out=b2[:, PACK * s : PACK * (s + 1)], in_=bias_raw[s][:])
+
+        def spread_small_vectors():
             for i, dest in enumerate((be_all, g_all)):
-                spread = work_pool.tile([P, D], F32, tag="work")
+                spread = y_pool.tile([P, D], F32, tag="y")
                 nc.tensor.matmul(
                     spread[:], lhsT=ones[:], rhs=row_zero[:, D * i : D * (i + 1)], start=True, stop=True
                 )
@@ -130,7 +137,6 @@ def tile_wavenetworklm_pb_kernel(tc, h_r, h_i, w2r, b2r, w2i, b2i, We, be, g_rms
         h_grouped = {}
         h_codes = {}
         h_scales = {}
-        acc = {}
         cat_plain = {}
         cat_grouped = {}
         cat_codes = {}
@@ -156,20 +162,32 @@ def tile_wavenetworklm_pb_kernel(tc, h_r, h_i, w2r, b2r, w2i, b2i, We, be, g_rms
                 in_=w_grouped[(matrix, g)][:],
             )
 
-        def flip_hidden(s, q):
-            words = h_raw[(s, q)][:].bitcast(F32)
-            grouped = stage.tile([P, PASSES * PACK * COLS], BF16, align_bytes=64, tag="h_grouped")
-            pairs = grouped[:].bitcast(F32).rearrange("p (g j r u) -> p g j r u", g=PASSES, j=TILES, u=2)
-            for g in range(PASSES):
-                flipped = work_pool.tile([P, TILES * 2, P], F32, tag="work")
-                for j in range(TILES):
+        def flip_tile(s, q, j):
+            if j == 0:
+                grouped = stage.tile(
+                    [P, PASSES * PACK * COLS], BF16, align_bytes=64, name="h_grouped", tag="h_grouped", bufs=LOOKAHEAD + 1
+                )
+                h_grouped[(s, q)] = grouped
+            pairs = h_grouped[(s, q)][:].bitcast(F32).rearrange("p (g j r u) -> p j g r u", g=PASSES, j=TILES, u=2)
+            words = h_raw[(s, TILES * q + j)][:].bitcast(F32)
+            for first_pass in range(0, PASSES, PAIR_PASSES):
+                flipped = flip_pool.tile([P, PAIR_PASSES * 2, P], F32, tag="flip")
+                for i in range(PAIR_PASSES):
+                    first = (first_pass + i) * (K_PASS // 2)
                     for u in range(2):
-                        first = j * WORDS + g * (K_PASS // 2)
                         nc.tensor.transpose(
-                            flipped[:, 2 * j + u, :], words[:, first + u : first + K_PASS // 2 : 2], ident_f32[:]
+                            flipped[:, 2 * i + u, :],
+                            words[:, first + u : first + K_PASS // 2 : 2],
+                            ident_f32[:],
                         )
-                nc.scalar.copy(out=pairs[:, g], in_=flipped[:].rearrange("p (j u) r -> p j r u", u=2))
-            h_grouped[(s, q)] = grouped
+                nc.scalar.copy(
+                    out=pairs[:, j, first_pass : first_pass + PAIR_PASSES],
+                    in_=flipped[:].rearrange("p (i u) r -> p i r u", u=2),
+                )
+
+        def flip_hidden(s, q):
+            for j in range(TILES):
+                flip_tile(s, q, j)
 
         def quantise_hidden(s, q):
             codes = stage.tile([P, PASSES * COLS], U32, align_bytes=64, tag="h_codes")
@@ -178,86 +196,91 @@ def tile_wavenetworklm_pb_kernel(tc, h_r, h_i, w2r, b2r, w2i, b2i, We, be, g_rms
             h_codes[(s, q)] = codes
             h_scales[(s, q)] = scales
 
-        def first_stage(s, q):
+        def multiply(acc, s, q, m, g, first_tile, tiles):
+            rows = slice(P * m, P * (m + 1))
+            cols = slice(COLS * g + P * first_tile, COLS * g + P * (first_tile + tiles))
+            nc.tensor.matmul_mx(
+                out=acc[:],
+                lhsT=w_codes[s][:, g, rows].bitcast(FP8X4),
+                lhsT_scale=w_scales[s][:, g, rows],
+                rhs=h_codes[(s, q)][:, cols].bitcast(FP8X4),
+                rhs_scale=h_scales[(s, q)][:, cols],
+                start=(g == 0),
+                stop=(g == PASSES - 1),
+            )
+
+        def add_first_bias(acc, s, q, m, first_tile, tiles):
+            if m == 0:
+                plain = stage.tile([P, D_TILES * COLS], BF16, tag="cat_plain")
+                cat_plain[(s, q, first_tile)] = plain
+            width = P * tiles
+            nc.scalar.activation(
+                out=cat_plain[(s, q, first_tile)][:, width * m : width * (m + 1)],
+                in_=acc[:],
+                func=ACT.Identity,
+                bias=b2[:, D_TILES * s + m : D_TILES * s + m + 1],
+                scale=1.0,
+            )
+
+        def first_stage(s, q, first_tile, tiles):
             for m in range(D_TILES):
-                acc[m] = acc_pool.tile([P, COLS], F32, name="acc_%d" % m)
-                rows = slice(P * m, P * (m + 1))
+                acc = acc_pool.tile([P, P * tiles], F32, tag="acc")
                 for g in range(PASSES):
-                    cols = slice(COLS * g, COLS * (g + 1))
-                    nc.tensor.matmul_mx(
-                        out=acc[m][:],
-                        lhsT=w_codes[s][:, g, rows].bitcast(FP8X4),
-                        lhsT_scale=w_scales[s][:, g, rows],
-                        rhs=h_codes[(s, q)][:, cols].bitcast(FP8X4),
-                        rhs_scale=h_scales[(s, q)][:, cols],
-                        start=(g == 0),
-                        stop=(g == PASSES - 1),
-                    )
+                    multiply(acc, s, q, m, g, first_tile, tiles)
+                add_first_bias(acc, s, q, m, first_tile, tiles)
 
-        def add_first_bias(s, q):
-            plain = stage.tile([P, D_TILES * COLS], BF16, tag="cat_plain")
-            for m in range(D_TILES):
-                nc.scalar.activation(
-                    out=plain[:, COLS * m : COLS * (m + 1)],
-                    in_=acc[m][:],
-                    func=ACT.Identity,
-                    bias=b2[:, D_TILES * s + m : D_TILES * s + m + 1],
-                    scale=1.0,
-                )
-            cat_plain[(s, q)] = plain
-
-        def regroup_cat(s, q):
+        def regroup_cat(s, q, first_tile, tiles):
+            size = PACK * P * tiles
             grouped = stage.tile([P, PACK * COLS], BF16, align_bytes=64, tag="cat_grouped")
-            regroup(nc, grouped[:], cat_plain[(s, q)][:])
-            cat_grouped[(s, q)] = grouped
+            regroup(nc, grouped[:, 0:size], cat_plain[(s, q, first_tile)][:, 0:size])
+            cat_grouped[(s, q, first_tile)] = grouped
 
-        def quantise_cat(s, q):
-            codes = keep.tile([P, COLS], U32, align_bytes=64, name="cat_codes_%d_%d" % (s, q))
-            scales = keep.tile([P, COLS], U8, align_bytes=64, name="cat_scales_%d_%d" % (s, q))
-            nc.vector.quantize_mx(out=codes[:].bitcast(FP8X4), scales=scales[:], in_=cat_grouped[(s, q)][:])
-            cat_codes[(s, q)] = codes
-            cat_scales[(s, q)] = scales
+        def quantise_cat(s, q, first_tile, tiles):
+            codes = keep.tile([P, P * tiles], U32, align_bytes=64, name="cat_codes_%d_%d_%d" % (s, q, first_tile))
+            scales = keep.tile([P, P * tiles], U8, align_bytes=64, name="cat_scales_%d_%d_%d" % (s, q, first_tile))
+            nc.vector.quantize_mx(
+                out=codes[:].bitcast(FP8X4),
+                scales=scales[:],
+                in_=cat_grouped[(s, q, first_tile)][:, 0 : PACK * P * tiles],
+            )
+            for j in range(tiles):
+                cat_codes[(s, q, first_tile + j)] = codes[:, P * j : P * (j + 1)]
+                cat_scales[(s, q, first_tile + j)] = scales[:, P * j : P * (j + 1)]
 
-        def second_stage(q):
-            for j in range(TILES):
-                cols = slice(P * j, P * (j + 1))
-                y = work_pool.tile([P, D], F32, tag="work")
-                for s in range(STREAMS):
-                    nc.tensor.matmul_mx(
-                        out=y[:],
-                        lhsT=cat_codes[(s, q)][:, cols].bitcast(FP8X4),
-                        lhsT_scale=cat_scales[(s, q)][:, cols],
-                        rhs=w_codes[2][:, s, :].bitcast(FP8X4),
-                        rhs_scale=w_scales[2][:, s, :],
-                        start=(s == 0),
-                        stop=(s == STREAMS - 1),
-                    )
-                y_banks[(q, j)] = y
-
-        def add_second_bias(q):
-            for j in range(TILES):
-                wave = tail.tile([P, D], F32, tag="wave", bufs=3 * TILES)
-                nc.vector.tensor_tensor(out=wave[:], in0=y_banks[(q, j)][:], in1=be_all[:], op=ALU.add)
-                waves[(q, j)] = wave
-
-        def sum_squares(q):
-            total = tail.tile([P, TILES], F32, tag="total")
-            for j in range(TILES):
-                squares = tail.tile([P, D], BF16, tag="squares")
-                nc.scalar.activation(
-                    out=squares[:], in_=waves[(q, j)][:], func=ACT.Square, accum_out=total[:, j : j + 1]
+        def second_stage(q, j):
+            y = y_pool.tile([P, D], F32, tag="y")
+            for s in range(STREAMS):
+                nc.tensor.matmul_mx(
+                    out=y[:],
+                    lhsT=cat_codes[(s, q, j)].bitcast(FP8X4),
+                    lhsT_scale=cat_scales[(s, q, j)],
+                    rhs=w_codes[2][:, s, :].bitcast(FP8X4),
+                    rhs_scale=w_scales[2][:, s, :],
+                    start=(s == 0),
+                    stop=(s == STREAMS - 1),
                 )
-            totals[q] = total
+            y_banks[(q, j)] = y
 
-        def root_mean_square(q):
-            rms = tail.tile([P, TILES], F32, tag="rms")
-            nc.scalar.activation(out=rms[:], in_=totals[q][:], func=ACT.Sqrt, bias=eps[:], scale=1.0 / D)
-            roots[q] = rms
+        def add_second_bias(q, j):
+            wave = tail.tile([P, D], F32, tag="wave", bufs=3 * TILES)
+            nc.vector.tensor_tensor(out=wave[:], in0=y_banks[(q, j)][:], in1=be_all[:], op=ALU.add)
+            waves[(q, j)] = wave
 
-        def invert_rms(q):
-            inv = tail.tile([P, TILES], F32, tag="inv")
-            nc.vector.reciprocal(out=inv[:], in_=roots[q][:])
-            inverses[q] = inv
+        def sum_squares(q, j):
+            total = tail.tile([P, 1], F32, tag="total", bufs=2 * TILES)
+            squares = tail.tile([P, D], BF16, tag="squares", bufs=2)
+            nc.scalar.activation(out=squares[:], in_=waves[(q, j)][:], func=ACT.Square, accum_out=total[:])
+            totals[(q, j)] = total
+
+        def root_mean_square(q, j):
+            rms = tail.tile([P, 1], F32, tag="rms", bufs=2 * TILES)
+            nc.scalar.activation(out=rms[:], in_=totals[(q, j)][:], func=ACT.Sqrt, bias=eps[:], scale=1.0 / D)
+            roots[(q, j)] = rms
+
+        def invert_rms(q, j):
+            inv = tail.tile([P, 1], F32, tag="inv", bufs=2 * TILES)
+            nc.vector.reciprocal(out=inv[:], in_=roots[(q, j)][:])
+            inverses[(q, j)] = inv
 
         out_view = out.flatten_outer_dims().rearrange("(p j) d -> p j d", j=TOKEN_TILES)
 
@@ -266,7 +289,7 @@ def tile_wavenetworklm_pb_kernel(tc, h_r, h_i, w2r, b2r, w2i, b2i, We, be, g_rms
             nc.vector.scalar_tensor_tensor(
                 out=normed[:],
                 in0=waves[(q, j)][:],
-                scalar=inverses[q][:, j : j + 1],
+                scalar=inverses[(q, j)][:],
                 in1=g_all[:],
                 op0=ALU.mult,
                 op1=ALU.mult,
@@ -279,38 +302,81 @@ def tile_wavenetworklm_pb_kernel(tc, h_r, h_i, w2r, b2r, w2i, b2i, We, be, g_rms
         def quarter_at(i):
             return [q for s, q in unit_at(i) if s == STREAMS - 1]
 
-        for step in range(FIRST_STEP, len(units) + 3):
-            chunks = chunks_of_step(step)
+        first = units[0]
+        second = units[1]
+        flip_tile(*first, 0)
+        flip_tile(*first, 1)
+        regroup_chunk(0, 0)
+        quantise_chunk(0, 0)
+        regroup_chunk(0, 1)
+        quantise_hidden(*first)
+        quantise_chunk(0, 1)
+        spread_small_vectors()
+        flip_tile(*second, 0)
+        sums = []
+        for m in range(D_TILES):
+            if m < D_TILES - 1:
+                acc = acc_pool.tile([P, COLS], F32, tag="acc")
+            else:
+                acc = y_pool.tile([P, COLS], F32, tag="y")
+            sums.append(acc)
+        for g in range(PASSES):
+            if g >= 2:
+                regroup_chunk(0, g)
+                if g == 2:
+                    widen_first_bias()
+                quantise_chunk(0, g)
+            for m in range(D_TILES):
+                multiply(sums[m], *first, m, g, 0, TILES)
+            if g == 1:
+                flip_tile(*second, 1)
+        quantise_hidden(*second)
+        for m in range(D_TILES):
+            add_first_bias(sums[m], *first, m, 0, TILES)
+        flip_hidden(*units[2])
+
+        chunks_of_step = {1: [(1, 0), (1, 1)], 2: [(1, 2)], 3: [(1, 3)], 4: [(2, 0), (2, 1)]}
+
+        def parts_of(i):
+            return [(0, TILES)] if i < len(units) - 1 else [(j, 1) for j in range(TILES)]
+
+        for step in range(1, len(units) + 3):
+            chunks = chunks_of_step.get(step, [])
             for q in quarter_at(step - 2):
-                add_second_bias(q)
-            for s, q in unit_at(step + 1):
-                flip_hidden(s, q)
-            for q in quarter_at(step - 3):
-                invert_rms(q)
+                for j in range(TILES):
+                    add_second_bias(q, j)
             for s, q in unit_at(step - 1):
-                regroup_cat(s, q)
+                for part in parts_of(step - 1):
+                    regroup_cat(s, q, *part)
             for i, chunk in enumerate(chunks):
                 regroup_chunk(*chunk)
-                if i > 0:
+                if i == 0:
+                    for s, q in unit_at(step - 1):
+                        for part in parts_of(step - 1):
+                            quantise_cat(s, q, *part)
+                else:
                     quantise_chunk(*chunks[i - 1])
-            for q in quarter_at(step - 3):
-                normalise_tile(q, 0)
-            for s, q in unit_at(step - 1):
-                quantise_cat(s, q)
-            for q in quarter_at(step - 3):
-                normalise_tile(q, 1)
-            for chunk in chunks[-1:]:
-                quantise_chunk(*chunk)
-            if step == FIRST_STEP:
-                spread_small_vectors()
-            for q in quarter_at(step - 2):
-                sum_squares(q)
-            for s, q in unit_at(step):
-                first_stage(s, q)
-                add_first_bias(s, q)
-            for q in quarter_at(step - 1):
-                second_stage(q)
-            for q in quarter_at(step - 2):
-                root_mean_square(q)
+            if not chunks:
+                for s, q in unit_at(step - 1):
+                    for part in parts_of(step - 1):
+                        quantise_cat(s, q, *part)
             for s, q in unit_at(step + 1):
                 quantise_hidden(s, q)
+            for chunk in chunks[-1:]:
+                quantise_chunk(*chunk)
+            for s, q in unit_at(step):
+                for part in parts_of(step):
+                    first_stage(s, q, *part)
+            for q in quarter_at(step - 1):
+                for j in range(TILES):
+                    second_stage(q, j)
+            for q in quarter_at(step - 3):
+                for j in range(TILES):
+                    invert_rms(q, j)
+                    normalise_tile(q, j)
+            for q in quarter_at(step - 2):
+                for j in range(TILES):
+                    sum_squares(q, j)
+                    root_mean_square(q, j)
+            for s, q in unit_at(step + LOOKAHEAD):
+                flip_hidden(s, q)

@@ -66,7 +66,7 @@ def tile_wavenetworklm_pb_kernel(tc, h_r, h_i, w2r, b2r, w2i, b2i, We, be, g_rms
         w_raw = {}
 
         def load_hidden(s, tile):
-            view = hidden[s].flatten_outer_dims().rearrange("(p j) k -> j p k", j=TOKEN_TILES)
+            view = hidden[s].flatten_outer_dims().rearrange("(j p) k -> j p k", p=P)
             rows = raw.tile([P, F], BF16, name="h_raw_%d_%d" % (s, tile))
             nc.sync.dma_start(out=rows[:], in_=view[tile])
             h_raw[(s, tile)] = rows
@@ -282,7 +282,7 @@ def tile_wavenetworklm_pb_kernel(tc, h_r, h_i, w2r, b2r, w2i, b2i, We, be, g_rms
             nc.vector.reciprocal(out=inv[:], in_=roots[(q, j)][:])
             inverses[(q, j)] = inv
 
-        out_view = out.flatten_outer_dims().rearrange("(p j) d -> p j d", j=TOKEN_TILES)
+        out_view = out.flatten_outer_dims().rearrange("(j p) d -> j p d", p=P)
 
         def normalise_tile(q, j):
             normed = tail.tile([P, D], F32, tag="normed", bufs=2 * TILES)
@@ -294,7 +294,7 @@ def tile_wavenetworklm_pb_kernel(tc, h_r, h_i, w2r, b2r, w2i, b2i, We, be, g_rms
                 op0=ALU.mult,
                 op1=ALU.mult,
             )
-            nc.sync.dma_start(out=out_view[:, TILES * q + j, :], in_=normed[:])
+            nc.sync.dma_start(out=out_view[TILES * q + j], in_=normed[:])
 
         def unit_at(i):
             return [units[i]] if 0 <= i < len(units) else []

@@ -32,16 +32,16 @@ LOOKAHEAD = 2
 FLOPS = 2 * TOKENS * F * D * STREAMS + 2 * TOKENS * (STREAMS * D) * D
 
 
-def regroup(nc, grouped, rows):
+def regroup(copy, grouped, rows, first, last):
     src = rows.rearrange("p (t c i) -> p c t i", t=PACK, i=4)
     dst = grouped.rearrange("p (c i t) -> p c t i", i=4, t=PACK)
-    nc.vector.tensor_copy(out=dst, in_=src)
+    copy(out=dst[:, first // 4 : last // 4], in_=src[:, first // 4 : last // 4])
 
 
-def regroup_by_channel(nc, grouped, rows):
+def regroup_by_channel(copy, grouped, rows, first, last):
     src = rows.rearrange("p (j m t) -> p m j t", j=PACK, t=PACK)
     dst = grouped.rearrange("p (t m j) -> p m j t", t=PACK, j=PACK)
-    nc.vector.tensor_copy(out=dst, in_=src)
+    copy(out=dst[:, first // 4 : last // 4], in_=src[:, first // 4 : last // 4])
 
 
 def tile_wavenetworklm_pb_kernel(tc, h_r, h_i, w2r, b2r, w2i, b2i, We, be, g_rms, out):
@@ -58,9 +58,8 @@ def tile_wavenetworklm_pb_kernel(tc, h_r, h_i, w2r, b2r, w2i, b2i, We, be, g_rms
         keep = ctx.enter_context(tc.tile_pool(name="keep", bufs=1))
         stage = ctx.enter_context(tc.tile_pool(name="stage", bufs=2))
         tail = ctx.enter_context(tc.tile_pool(name="tail", bufs=3))
-        acc_pool = ctx.enter_context(tc.psum_pool(name="acc", bufs=3))
-        flip_pool = ctx.enter_context(tc.psum_pool(name="flip", bufs=3))
-        y_pool = ctx.enter_context(tc.psum_pool(name="y", bufs=2))
+        acc_pool = ctx.enter_context(tc.psum_pool(name="acc", bufs=4))
+        flip_pool = ctx.enter_context(tc.psum_pool(name="flip", bufs=4))
 
         h_raw = {}
         w_raw = {}
@@ -87,15 +86,16 @@ def tile_wavenetworklm_pb_kernel(tc, h_r, h_i, w2r, b2r, w2i, b2i, We, be, g_rms
         for tile in range(3, 6):
             load_hidden(0, tile)
         load_chunk(1, 0)
+        load_chunk(1, 1)
         load_hidden(0, 6)
         load_hidden(0, 7)
-        for g in range(1, PASSES):
-            load_chunk(1, g)
-        for tile in range(0, 4):
+        load_chunk(1, 3)
+        load_chunk(1, 2)
+        for tile in range(0, 2):
             load_hidden(1, tile)
         for g in range(STREAMS):
             load_chunk(2, g)
-        for tile in range(4, TOKEN_TILES):
+        for tile in range(2, TOKEN_TILES):
             load_hidden(1, tile)
 
         bias_raw = [const.tile([P, PACK], BF16, name="bias_raw_%d" % s) for s in range(STREAMS)]
@@ -124,7 +124,7 @@ def tile_wavenetworklm_pb_kernel(tc, h_r, h_i, w2r, b2r, w2i, b2i, We, be, g_rms
 
         def spread_small_vectors():
             for i, dest in enumerate((be_all, g_all)):
-                spread = y_pool.tile([P, D], F32, tag="y")
+                spread = acc_pool.tile([P, D], F32, tag="acc")
                 nc.tensor.matmul(
                     spread[:], lhsT=ones[:], rhs=row_zero[:, D * i : D * (i + 1)], start=True, stop=True
                 )
@@ -147,13 +147,12 @@ def tile_wavenetworklm_pb_kernel(tc, h_r, h_i, w2r, b2r, w2i, b2i, We, be, g_rms
         roots = {}
         inverses = {}
 
-        def regroup_chunk(matrix, g):
-            grouped = stage.tile([P, PACK * D], BF16, align_bytes=64, tag="w_grouped", bufs=3)
-            if matrix < STREAMS:
-                regroup_by_channel(nc, grouped[:], w_raw[(matrix, g)][:])
-            else:
-                regroup(nc, grouped[:], w_raw[(matrix, g)][:])
-            w_grouped[(matrix, g)] = grouped
+        def regroup_chunk(matrix, g, copy=nc.vector.tensor_copy, first=0, last=D):
+            if first == 0:
+                grouped = stage.tile([P, PACK * D], BF16, align_bytes=64, tag="w_grouped", bufs=4)
+                w_grouped[(matrix, g)] = grouped
+            move = regroup_by_channel if matrix < STREAMS else regroup
+            move(copy, w_grouped[(matrix, g)][:], w_raw[(matrix, g)][:], first, last)
 
         def quantise_chunk(matrix, g):
             nc.vector.quantize_mx(
@@ -222,17 +221,19 @@ def tile_wavenetworklm_pb_kernel(tc, h_r, h_i, w2r, b2r, w2i, b2i, We, be, g_rms
                 scale=1.0,
             )
 
-        def first_stage(s, q, first_tile, tiles):
+        def first_stage(s, q, first_tile, tiles, fillers):
             for m in range(D_TILES):
                 acc = acc_pool.tile([P, P * tiles], F32, tag="acc")
                 for g in range(PASSES):
                     multiply(acc, s, q, m, g, first_tile, tiles)
                 add_first_bias(acc, s, q, m, first_tile, tiles)
+                for filler in fillers[m : m + 1]:
+                    filler()
 
         def regroup_cat(s, q, first_tile, tiles):
             size = PACK * P * tiles
             grouped = stage.tile([P, PACK * COLS], BF16, align_bytes=64, tag="cat_grouped")
-            regroup(nc, grouped[:, 0:size], cat_plain[(s, q, first_tile)][:, 0:size])
+            regroup(nc.vector.tensor_copy, grouped[:, 0:size], cat_plain[(s, q, first_tile)][:, 0:size], 0, P * tiles)
             cat_grouped[(s, q, first_tile)] = grouped
 
         def quantise_cat(s, q, first_tile, tiles):
@@ -248,7 +249,7 @@ def tile_wavenetworklm_pb_kernel(tc, h_r, h_i, w2r, b2r, w2i, b2i, We, be, g_rms
                 cat_scales[(s, q, first_tile + j)] = scales[:, P * j : P * (j + 1)]
 
         def second_stage(q, j):
-            y = y_pool.tile([P, D], F32, tag="y")
+            y = acc_pool.tile([P, D], F32, tag="acc")
             for s in range(STREAMS):
                 nc.tensor.matmul_mx(
                     out=y[:],
@@ -305,78 +306,100 @@ def tile_wavenetworklm_pb_kernel(tc, h_r, h_i, w2r, b2r, w2i, b2i, We, be, g_rms
         first = units[0]
         second = units[1]
         flip_tile(*first, 0)
+        spread_small_vectors()
         flip_tile(*first, 1)
         regroup_chunk(0, 0)
         quantise_chunk(0, 0)
         regroup_chunk(0, 1)
+        regroup_chunk(0, 2, nc.scalar.copy)
         quantise_hidden(*first)
         quantise_chunk(0, 1)
-        spread_small_vectors()
         flip_tile(*second, 0)
         sums = []
         for m in range(D_TILES):
-            if m < D_TILES - 1:
-                acc = acc_pool.tile([P, COLS], F32, tag="acc")
-            else:
-                acc = y_pool.tile([P, COLS], F32, tag="y")
+            acc = acc_pool.tile([P, COLS], F32, tag="acc")
             sums.append(acc)
         for g in range(PASSES):
-            if g >= 2:
-                regroup_chunk(0, g)
-                if g == 2:
-                    widen_first_bias()
-                quantise_chunk(0, g)
+            if g == 2:
+                regroup_chunk(0, 3)
+                quantise_chunk(0, 2)
+                widen_first_bias()
+                quantise_chunk(0, 3)
             for m in range(D_TILES):
                 multiply(sums[m], *first, m, g, 0, TILES)
             if g == 1:
                 flip_tile(*second, 1)
-        quantise_hidden(*second)
         for m in range(D_TILES):
             add_first_bias(sums[m], *first, m, 0, TILES)
-        flip_hidden(*units[2])
 
-        chunks_of_step = {1: [(1, 0), (1, 1)], 2: [(1, 2)], 3: [(1, 3)], 4: [(2, 0), (2, 1)]}
+        def each_tile(work, q):
+            for j in range(TILES):
+                work(q, j)
 
-        def parts_of(i):
-            return [(0, TILES)] if i < len(units) - 1 else [(j, 1) for j in range(TILES)]
+        def norms_of(q):
+            return [
+                lambda: None,
+                lambda: sum_squares(q, 0),
+                lambda: sum_squares(q, 1),
+                lambda: each_tile(root_mean_square, q),
+            ]
 
-        for step in range(1, len(units) + 3):
-            chunks = chunks_of_step.get(step, [])
-            for q in quarter_at(step - 2):
-                for j in range(TILES):
-                    add_second_bias(q, j)
-            for s, q in unit_at(step - 1):
-                for part in parts_of(step - 1):
-                    regroup_cat(s, q, *part)
-            for i, chunk in enumerate(chunks):
+        def by_scalar(chunk, first, last, pieces):
+            step = (last - first) // pieces
+            return [lambda c=c: regroup_chunk(*chunk, nc.scalar.copy, c, c + step) for c in range(first, last, step)]
+
+        own = {0: [(1, 0)], 1: [(1, 3)], 2: [(2, 0)]}
+        shared = {1: [(1, 1)], 2: [(1, 2)], 3: [(2, 1)]}
+        HALF = D // 2
+        quantise_hidden(*second)
+        for step in range(0, len(units) - 1):
+            s, q = units[step]
+            fillers = []
+            if step > 0:
+                quantise_hidden(*units[step + 1])
+            for chunk in own.get(step, []):
                 regroup_chunk(*chunk)
-                if i == 0:
-                    for s, q in unit_at(step - 1):
-                        for part in parts_of(step - 1):
-                            quantise_cat(s, q, *part)
-                else:
-                    quantise_chunk(*chunks[i - 1])
-            if not chunks:
-                for s, q in unit_at(step - 1):
-                    for part in parts_of(step - 1):
-                        quantise_cat(s, q, *part)
-            for s, q in unit_at(step + 1):
-                quantise_hidden(s, q)
-            for chunk in chunks[-1:]:
+            for chunk in shared.get(step, []):
+                fillers = by_scalar(chunk, 0, HALF, D_TILES)
+            for done in quarter_at(step - 2):
+                fillers = norms_of(done)
+            if step > 0:
+                first_stage(s, q, 0, TILES, fillers)
+            for chunk in shared.get(step, []):
+                regroup_chunk(*chunk, nc.vector.tensor_copy, HALF, D)
+            for done in quarter_at(step - 1):
+                each_tile(second_stage, done)
+                add_second_bias(done, 0)
+            regroup_cat(s, q, 0, TILES)
+            for chunk in own.get(step, []):
                 quantise_chunk(*chunk)
-            for s, q in unit_at(step):
-                for part in parts_of(step):
-                    first_stage(s, q, *part)
-            for q in quarter_at(step - 1):
-                for j in range(TILES):
-                    second_stage(q, j)
-            for q in quarter_at(step - 3):
-                for j in range(TILES):
-                    invert_rms(q, j)
-                    normalise_tile(q, j)
-            for q in quarter_at(step - 2):
-                for j in range(TILES):
-                    sum_squares(q, j)
-                    root_mean_square(q, j)
-            for s, q in unit_at(step + LOOKAHEAD):
-                flip_hidden(s, q)
+            for done in quarter_at(step - 1):
+                add_second_bias(done, 1)
+            for done in quarter_at(step - 2):
+                each_tile(invert_rms, done)
+            quantise_cat(s, q, 0, TILES)
+            for chunk in shared.get(step, []):
+                quantise_chunk(*chunk)
+            for ahead in unit_at(step + LOOKAHEAD):
+                flip_hidden(*ahead)
+            for done in quarter_at(step - 2):
+                each_tile(normalise_tile, done)
+        s, q = units[-1]
+        first_stage(s, q, 0, TILES, norms_of(q - 2))
+        each_tile(second_stage, q - 1)
+        add_second_bias(q - 1, 0)
+        regroup_cat(s, q, 0, TILES)
+        each_tile(invert_rms, q - 2)
+        add_second_bias(q - 1, 1)
+        quantise_cat(s, q, 0, TILES)
+        each_tile(sum_squares, q - 1)
+        each_tile(root_mean_square, q - 1)
+        each_tile(second_stage, q)
+        each_tile(normalise_tile, q - 2)
+        each_tile(add_second_bias, q)
+        each_tile(sum_squares, q)
+        each_tile(invert_rms, q - 1)
+        each_tile(root_mean_square, q)
+        each_tile(normalise_tile, q - 1)
+        each_tile(invert_rms, q)
+        each_tile(normalise_tile, q)

@@ -109,18 +109,13 @@ def tile_wavenetworklm_pb_kernel(tc, h_r, h_i, w2r, b2r, w2i, b2i, We, be, g_rms
         eps = const.tile([P, 1], F32)
         nc.vector.memset(eps[:], EPS)
         warm = const.tile([P, 1], F32)
-        nc.scalar.activation(out=warm[:], in_=eps[:], func=ACT.Sqrt)
+        nc.scalar.activation(out=warm[:], in_=eps[:], func=ACT.Abs_reciprocal_sqrt)
         ident_f32 = const.tile([P, P], F32)
         make_identity(nc, ident_f32[:])
         ones = const.tile([P, P], BF16)
         nc.vector.memset(ones[:], 1.0)
-        b2 = const.tile([P, STREAMS * D_TILES], F32)
         be_all = const.tile([P, D], F32)
         g_all = const.tile([P, D], F32)
-
-        def widen_first_bias():
-            for s in range(STREAMS):
-                nc.vector.tensor_copy(out=b2[:, PACK * s : PACK * (s + 1)], in_=bias_raw[s][:])
 
         def spread_small_vectors():
             for i, dest in enumerate((be_all, g_all)):
@@ -144,7 +139,6 @@ def tile_wavenetworklm_pb_kernel(tc, h_r, h_i, w2r, b2r, w2i, b2i, We, be, g_rms
         y_banks = {}
         waves = {}
         totals = {}
-        roots = {}
         inverses = {}
 
         def regroup_chunk(matrix, g, copy=nc.vector.tensor_copy, first=0, last=D):
@@ -217,7 +211,7 @@ def tile_wavenetworklm_pb_kernel(tc, h_r, h_i, w2r, b2r, w2i, b2i, We, be, g_rms
                 out=cat_plain[(s, q, first_tile)][:, width * m : width * (m + 1)],
                 in_=acc[:],
                 func=ACT.Identity,
-                bias=b2[:, D_TILES * s + m : D_TILES * s + m + 1],
+                bias=bias_raw[s][:, m : m + 1],
                 scale=1.0,
             )
 
@@ -268,20 +262,20 @@ def tile_wavenetworklm_pb_kernel(tc, h_r, h_i, w2r, b2r, w2i, b2i, We, be, g_rms
             waves[(q, j)] = wave
 
         def sum_squares(q, j):
-            total = tail.tile([P, 1], F32, tag="total", bufs=2 * TILES)
+            if j == 0:
+                total = tail.tile([P, TILES], F32, tag="total")
+                totals[q] = total
             squares = tail.tile([P, D], BF16, tag="squares", bufs=2)
-            nc.scalar.activation(out=squares[:], in_=waves[(q, j)][:], func=ACT.Square, accum_out=total[:])
-            totals[(q, j)] = total
+            nc.scalar.activation(
+                out=squares[:], in_=waves[(q, j)][:], func=ACT.Square, accum_out=totals[q][:, j : j + 1]
+            )
 
-        def root_mean_square(q, j):
-            rms = tail.tile([P, 1], F32, tag="rms", bufs=2 * TILES)
-            nc.scalar.activation(out=rms[:], in_=totals[(q, j)][:], func=ACT.Sqrt, bias=eps[:], scale=1.0 / D)
-            roots[(q, j)] = rms
-
-        def invert_rms(q, j):
-            inv = tail.tile([P, 1], F32, tag="inv", bufs=2 * TILES)
-            nc.vector.reciprocal(out=inv[:], in_=roots[(q, j)][:])
-            inverses[(q, j)] = inv
+        def invert_rms(q):
+            inv = tail.tile([P, TILES], F32, tag="inv")
+            nc.scalar.activation(
+                out=inv[:], in_=totals[q][:], func=ACT.Abs_reciprocal_sqrt, bias=eps[:], scale=1.0 / D
+            )
+            inverses[q] = inv
 
         out_view = out.flatten_outer_dims().rearrange("(j p) d -> j p d", p=P)
 
@@ -290,7 +284,7 @@ def tile_wavenetworklm_pb_kernel(tc, h_r, h_i, w2r, b2r, w2i, b2i, We, be, g_rms
             nc.vector.scalar_tensor_tensor(
                 out=normed[:],
                 in0=waves[(q, j)][:],
-                scalar=inverses[(q, j)][:],
+                scalar=inverses[q][:, j : j + 1],
                 in1=g_all[:],
                 op0=ALU.mult,
                 op1=ALU.mult,
@@ -323,7 +317,6 @@ def tile_wavenetworklm_pb_kernel(tc, h_r, h_i, w2r, b2r, w2i, b2i, We, be, g_rms
             if g == 2:
                 regroup_chunk(0, 3)
                 quantise_chunk(0, 2)
-                widen_first_bias()
                 quantise_chunk(0, 3)
             for m in range(D_TILES):
                 multiply(sums[m], *first, m, g, 0, TILES)
@@ -341,7 +334,7 @@ def tile_wavenetworklm_pb_kernel(tc, h_r, h_i, w2r, b2r, w2i, b2i, We, be, g_rms
                 lambda: None,
                 lambda: sum_squares(q, 0),
                 lambda: sum_squares(q, 1),
-                lambda: each_tile(root_mean_square, q),
+                lambda: invert_rms(q),
             ]
 
         def by_scalar(chunk, first, last, pieces):
@@ -375,8 +368,6 @@ def tile_wavenetworklm_pb_kernel(tc, h_r, h_i, w2r, b2r, w2i, b2i, We, be, g_rms
                 quantise_chunk(*chunk)
             for done in quarter_at(step - 1):
                 add_second_bias(done, 1)
-            for done in quarter_at(step - 2):
-                each_tile(invert_rms, done)
             quantise_cat(s, q, 0, TILES)
             for chunk in shared.get(step, []):
                 quantise_chunk(*chunk)
@@ -389,17 +380,14 @@ def tile_wavenetworklm_pb_kernel(tc, h_r, h_i, w2r, b2r, w2i, b2i, We, be, g_rms
         each_tile(second_stage, q - 1)
         add_second_bias(q - 1, 0)
         regroup_cat(s, q, 0, TILES)
-        each_tile(invert_rms, q - 2)
         add_second_bias(q - 1, 1)
         quantise_cat(s, q, 0, TILES)
         each_tile(sum_squares, q - 1)
-        each_tile(root_mean_square, q - 1)
+        invert_rms(q - 1)
         each_tile(second_stage, q)
         each_tile(normalise_tile, q - 2)
         each_tile(add_second_bias, q)
         each_tile(sum_squares, q)
-        each_tile(invert_rms, q - 1)
-        each_tile(root_mean_square, q)
+        invert_rms(q)
         each_tile(normalise_tile, q - 1)
-        each_tile(invert_rms, q)
         each_tile(normalise_tile, q)

@@ -97,14 +97,14 @@ def tile_wavenetworklm_pb_kernel(tc, h_r, h_i, w2r, b2r, w2i, b2i, We, be, g_rms
             load_chunk(2, g)
         for tile in range(2, TOKEN_TILES):
             load_hidden(1, tile)
+        be_all = const.tile([P, D], BF16)
+        nc.sync.dma_start(out=be_all[:], in_=be.partition_broadcast(P))
+        g_all = const.tile([P, D], BF16)
+        nc.sync.dma_start(out=g_all[:], in_=g_rms.partition_broadcast(P))
 
         bias_raw = [const.tile([P, PACK], BF16, name="bias_raw_%d" % s) for s in range(STREAMS)]
         for s in range(STREAMS):
             nc.scalar.dma_start(out=bias_raw[s][:], in_=biases[s].rearrange("(p t) -> p t", t=PACK))
-        row_zero = const.tile([P, 2 * D], BF16)
-        nc.vector.memset(row_zero[:], 0.0)
-        nc.scalar.dma_start(out=row_zero[0:1, 0:D], in_=be.rearrange("(o n) -> o n", o=1))
-        nc.scalar.dma_start(out=row_zero[0:1, D : 2 * D], in_=g_rms.rearrange("(o n) -> o n", o=1))
 
         eps = const.tile([P, 1], F32)
         nc.vector.memset(eps[:], EPS)
@@ -112,19 +112,6 @@ def tile_wavenetworklm_pb_kernel(tc, h_r, h_i, w2r, b2r, w2i, b2i, We, be, g_rms
         nc.scalar.activation(out=warm[:], in_=eps[:], func=ACT.Abs_reciprocal_sqrt)
         ident_f32 = const.tile([P, P], F32)
         make_identity(nc, ident_f32[:])
-        ones = const.tile([P, P], BF16)
-        nc.vector.memset(ones[:], 1.0)
-        be_all = const.tile([P, D], F32)
-        g_all = const.tile([P, D], F32)
-
-        def spread_small_vectors():
-            for i, dest in enumerate((be_all, g_all)):
-                spread = acc_pool.tile([P, D], F32, tag="acc")
-                nc.tensor.matmul(
-                    spread[:], lhsT=ones[:], rhs=row_zero[:, D * i : D * (i + 1)], start=True, stop=True
-                )
-                nc.scalar.copy(out=dest[:], in_=spread[:])
-
         chunks_in = (PASSES, PASSES, STREAMS)
         w_codes = [keep.tile([P, n, D], U32, align_bytes=64, name="w_codes_%d" % i) for i, n in enumerate(chunks_in)]
         w_scales = [keep.tile([P, n, D], U8, align_bytes=64, name="w_scales_%d" % i) for i, n in enumerate(chunks_in)]
@@ -300,7 +287,6 @@ def tile_wavenetworklm_pb_kernel(tc, h_r, h_i, w2r, b2r, w2i, b2i, We, be, g_rms
         first = units[0]
         second = units[1]
         flip_tile(*first, 0)
-        spread_small_vectors()
         flip_tile(*first, 1)
         regroup_chunk(0, 0)
         quantise_chunk(0, 0)

@@ -117,6 +117,7 @@ def tile_wavenetworklm_pb_kernel(tc, h_r, h_i, w2r, b2r, w2i, b2i, We, be, g_rms
         w_scales = [keep.tile([P, n, D], U8, align_bytes=64, name="w_scales_%d" % i) for i, n in enumerate(chunks_in)]
         w_grouped = {}
         h_grouped = {}
+        h_words = {}
         h_codes = {}
         h_scales = {}
         cat_plain = {}
@@ -150,20 +151,29 @@ def tile_wavenetworklm_pb_kernel(tc, h_r, h_i, w2r, b2r, w2i, b2i, We, be, g_rms
                 h_grouped[(s, q)] = grouped
             pairs = h_grouped[(s, q)][:].bitcast(F32).rearrange("p (g j r u) -> p j g r u", g=PASSES, j=TILES, u=2)
             words = h_raw[(s, TILES * q + j)][:].bitcast(F32)
+            in_order = h_words.get((s, q, j))
             for first_pass in range(0, PASSES, PAIR_PASSES):
                 flipped = flip_pool.tile([P, PAIR_PASSES * 2, P], F32, tag="flip")
                 for i in range(PAIR_PASSES):
                     first = (first_pass + i) * (K_PASS // 2)
                     for u in range(2):
-                        nc.tensor.transpose(
-                            flipped[:, 2 * i + u, :],
-                            words[:, first + u : first + K_PASS // 2 : 2],
-                            ident_f32[:],
-                        )
+                        if in_order is None:
+                            pick = words[:, first + u : first + K_PASS // 2 : 2]
+                        else:
+                            pick = in_order[:, first + P * u : first + P * (u + 1)]
+                        nc.tensor.transpose(flipped[:, 2 * i + u, :], pick, ident_f32[:])
                 nc.scalar.copy(
                     out=pairs[:, j, first_pass : first_pass + PAIR_PASSES],
                     in_=flipped[:].rearrange("p (i u) r -> p i r u", u=2),
                 )
+
+        def order_words(s, q, j):
+            in_order = stage.tile([P, F // 2], F32, tag="in_order", bufs=TILES)
+            h_words[(s, q, j)] = in_order
+            nc.vector.tensor_copy(
+                out=in_order[:].rearrange("p (g u n) -> p g u n", g=PASSES, u=2),
+                in_=h_raw[(s, TILES * q + j)][:].bitcast(F32).rearrange("p (g n u) -> p g u n", g=PASSES, u=2),
+            )
 
         def flip_hidden(s, q):
             for j in range(TILES):
@@ -257,26 +267,35 @@ def tile_wavenetworklm_pb_kernel(tc, h_r, h_i, w2r, b2r, w2i, b2i, We, be, g_rms
                 out=squares[:], in_=waves[(q, j)][:], func=ACT.Square, accum_out=totals[q][:, j : j + 1]
             )
 
-        def invert_rms(q):
-            inv = tail.tile([P, TILES], F32, tag="inv")
+        def invert_rms(q, first_tile, tiles):
+            if first_tile == 0:
+                inv = tail.tile([P, TILES], F32, tag="inv")
+                inverses[q] = inv
+            cols = slice(first_tile, first_tile + tiles)
             nc.scalar.activation(
-                out=inv[:], in_=totals[q][:], func=ACT.Abs_reciprocal_sqrt, bias=eps[:], scale=1.0 / D
+                out=inverses[q][:, cols],
+                in_=totals[q][:, cols],
+                func=ACT.Abs_reciprocal_sqrt,
+                bias=eps[:],
+                scale=1.0 / D,
             )
-            inverses[q] = inv
 
         out_view = out.flatten_outer_dims().rearrange("(j p) d -> j p d", p=P)
 
-        def normalise_tile(q, j):
-            normed = tail.tile([P, D], F32, tag="normed", bufs=2 * TILES)
-            nc.vector.scalar_tensor_tensor(
-                out=normed[:],
-                in0=waves[(q, j)][:],
-                scalar=inverses[q][:, j : j + 1],
-                in1=g_all[:],
-                op0=ALU.mult,
-                op1=ALU.mult,
-            )
-            nc.sync.dma_start(out=out_view[TILES * q + j], in_=normed[:])
+        def normalise_tile(q, j, pieces=1):
+            for i in range(pieces):
+                width = D // pieces
+                cols = slice(width * i, width * (i + 1))
+                normed = tail.tile([P, width], F32, tag="normed", bufs=TOKEN_TILES)
+                nc.vector.scalar_tensor_tensor(
+                    out=normed[:],
+                    in0=waves[(q, j)][:, cols],
+                    scalar=inverses[q][:, j : j + 1],
+                    in1=g_all[:, cols],
+                    op0=ALU.mult,
+                    op1=ALU.mult,
+                )
+                nc.sync.dma_start(out=out_view[TILES * q + j][:, cols], in_=normed[:])
 
         def unit_at(i):
             return [units[i]] if 0 <= i < len(units) else []
@@ -320,20 +339,22 @@ def tile_wavenetworklm_pb_kernel(tc, h_r, h_i, w2r, b2r, w2i, b2i, We, be, g_rms
                 lambda: None,
                 lambda: sum_squares(q, 0),
                 lambda: sum_squares(q, 1),
-                lambda: invert_rms(q),
+                lambda: invert_rms(q, 0, TILES),
             ]
 
         def by_scalar(chunk, first, last, pieces):
             step = (last - first) // pieces
             return [lambda c=c: regroup_chunk(*chunk, nc.scalar.copy, c, c + step) for c in range(first, last, step)]
 
-        own = {0: [(1, 0)], 1: [(1, 3)], 2: [(2, 0)]}
-        shared = {1: [(1, 1)], 2: [(1, 2)], 3: [(2, 1)]}
+        own = {0: [(1, 0)], 1: [(1, 1)], 2: [(1, 2), (1, 3)], 4: [(2, 0)]}
+        shared = {4: [(2, 1)]}
         HALF = D // 2
         quantise_hidden(*second)
         for step in range(0, len(units) - 1):
             s, q = units[step]
             fillers = []
+            if step == 5:
+                order_words(*units[7], 0)
             if step > 0:
                 quantise_hidden(*units[step + 1])
             for chunk in own.get(step, []):
@@ -369,11 +390,13 @@ def tile_wavenetworklm_pb_kernel(tc, h_r, h_i, w2r, b2r, w2i, b2i, We, be, g_rms
         add_second_bias(q - 1, 1)
         quantise_cat(s, q, 0, TILES)
         each_tile(sum_squares, q - 1)
-        invert_rms(q - 1)
+        invert_rms(q - 1, 0, TILES)
         each_tile(second_stage, q)
         each_tile(normalise_tile, q - 2)
         each_tile(add_second_bias, q)
-        each_tile(sum_squares, q)
-        invert_rms(q)
+        for j in range(TILES):
+            sum_squares(q, j)
+            invert_rms(q, j, 1)
         each_tile(normalise_tile, q - 1)
-        each_tile(normalise_tile, q)
+        normalise_tile(q, 0)
+        normalise_tile(q, 1, 2)

from contextlib import ExitStack

import concourse.mybir as mybir
from concourse.masks import make_identity

F32 = mybir.dt.float32
BF16 = mybir.dt.bfloat16
U32 = mybir.dt.uint32
U8 = mybir.dt.uint8
FP8X4 = mybir.dt.float8_e4m3fn_x4
ACT = mybir.ActivationFunctionType
ALU = mybir.AluOpType

P = 128
PACK = 4
K_PASS = P * PACK
TOKENS = 1024
F = 2048
D = 512
EPS = 1e-6

STREAMS = 2
PASSES = F // K_PASS
D_TILES = D // P
TOKEN_TILES = TOKENS // P
TILES = 2
QUARTERS = TOKEN_TILES // TILES
COLS = TILES * P
PAIR_PASSES = 2
LOOKAHEAD = 2

FLOPS = 2 * TOKENS * F * D * STREAMS + 2 * TOKENS * (STREAMS * D) * D


def regroup(copy, grouped, rows, first, last):
    src = rows.rearrange("p (t c i) -> p c t i", t=PACK, i=4)
    dst = grouped.rearrange("p (c i t) -> p c t i", i=4, t=PACK)
    copy(out=dst[:, first // 4 : last // 4], in_=src[:, first // 4 : last // 4])


def regroup_by_channel(copy, grouped, rows, first, last):
    src = rows.rearrange("p (j m t) -> p m j t", j=PACK, t=PACK)
    dst = grouped.rearrange("p (t m j) -> p m j t", t=PACK, j=PACK)
    copy(out=dst[:, first // 4 : last // 4], in_=src[:, first // 4 : last // 4])


def tile_wavenetworklm_pb_kernel(tc, h_r, h_i, w2r, b2r, w2i, b2i, We, be, g_rms, out):
    nc = tc.nc
    hidden = (h_r, h_i)
    matrices = (w2r, w2i, We)
    biases = (b2r, b2i)
    units = [(s, q) for s in range(STREAMS) for q in range(QUARTERS)]

    with ExitStack() as ctx:
        ctx.enter_context(tc.manual_schedule())
        const = ctx.enter_context(tc.tile_pool(name="const", bufs=1))
        raw = ctx.enter_context(tc.tile_pool(name="raw", bufs=1))
        keep = ctx.enter_context(tc.tile_pool(name="keep", bufs=1))
        stage = ctx.enter_context(tc.tile_pool(name="stage", bufs=2))
        tail = ctx.enter_context(tc.tile_pool(name="tail", bufs=3))
        acc_pool = ctx.enter_context(tc.psum_pool(name="acc", bufs=4))
        flip_pool = ctx.enter_context(tc.psum_pool(name="flip", bufs=4))

        h_raw = {}
        w_raw = {}

        def load_hidden(s, tile):
            view = hidden[s].flatten_outer_dims().rearrange("(j p) k -> j p k", p=P)
            rows = raw.tile([P, F], BF16, name="h_raw_%d_%d" % (s, tile))
            nc.sync.dma_start(out=rows[:], in_=view[tile])
            h_raw[(s, tile)] = rows

        def load_chunk(matrix, g):
            rows = raw.tile([P, PACK * D], BF16, name="w_raw_%d_%d" % (matrix, g))
            view = matrices[matrix].rearrange("(c p t) n -> c p (t n)", p=P, t=PACK)
            nc.sync.dma_start(out=rows[:], in_=view[g])
            w_raw[(matrix, g)] = rows

        load_hidden(0, 0)
        load_chunk(0, 0)
        load_hidden(0, 1)
        load_chunk(0, 1)
        load_chunk(0, 2)
        load_hidden(0, 2)
        load_chunk(0, 3)
        for tile in range(3, 6):
            load_hidden(0, tile)
        load_chunk(1, 0)
        load_chunk(1, 1)
        load_hidden(0, 6)
        load_hidden(0, 7)
        load_chunk(1, 3)
        load_chunk(1, 2)
        for tile in range(0, 2):
            load_hidden(1, tile)
        for g in range(STREAMS):
            load_chunk(2, g)
        for tile in range(2, TOKEN_TILES):
            load_hidden(1, tile)
        be_all = const.tile([P, D], BF16)
        nc.sync.dma_start(out=be_all[:], in_=be.partition_broadcast(P))
        g_all = const.tile([P, D], BF16)
        nc.sync.dma_start(out=g_all[:], in_=g_rms.partition_broadcast(P))

        bias_raw = [const.tile([P, PACK], BF16, name="bias_raw_%d" % s) for s in range(STREAMS)]
        for s in range(STREAMS):
            nc.scalar.dma_start(out=bias_raw[s][:], in_=biases[s].rearrange("(p t) -> p t", t=PACK))

        eps = const.tile([P, 1], F32)
        nc.vector.memset(eps[:], EPS)
        warm = const.tile([P, 1], F32)
        nc.scalar.activation(out=warm[:], in_=eps[:], func=ACT.Abs_reciprocal_sqrt)
        ident_f32 = const.tile([P, P], F32)
        make_identity(nc, ident_f32[:])
        chunks_in = (PASSES, PASSES, STREAMS)
        w_codes = [keep.tile([P, n, D], U32, align_bytes=64, name="w_codes_%d" % i) for i, n in enumerate(chunks_in)]
        w_scales = [keep.tile([P, n, D], U8, align_bytes=64, name="w_scales_%d" % i) for i, n in enumerate(chunks_in)]
        w_grouped = {}
        h_grouped = {}
        h_words = {}
        h_codes = {}
        h_scales = {}
        cat_plain = {}
        cat_grouped = {}
        cat_codes = {}
        cat_scales = {}
        y_banks = {}
        waves = {}
        totals = {}
        inverses = {}

        def regroup_chunk(matrix, g, copy=nc.vector.tensor_copy, first=0, last=D):
            if first == 0:
                grouped = stage.tile([P, PACK * D], BF16, align_bytes=64, tag="w_grouped", bufs=4)
                w_grouped[(matrix, g)] = grouped
            move = regroup_by_channel if matrix < STREAMS else regroup
            move(copy, w_grouped[(matrix, g)][:], w_raw[(matrix, g)][:], first, last)

        def quantise_chunk(matrix, g):
            nc.vector.quantize_mx(
                out=w_codes[matrix][:, g, :].bitcast(FP8X4),
                scales=w_scales[matrix][:, g, :],
                in_=w_grouped[(matrix, g)][:],
            )

        def flip_tile(s, q, j):
            if j == 0:
                grouped = stage.tile(
                    [P, PASSES * PACK * COLS], BF16, align_bytes=64, name="h_grouped", tag="h_grouped", bufs=LOOKAHEAD + 1
                )
                h_grouped[(s, q)] = grouped
            pairs = h_grouped[(s, q)][:].bitcast(F32).rearrange("p (g j r u) -> p j g r u", g=PASSES, j=TILES, u=2)
            words = h_raw[(s, TILES * q + j)][:].bitcast(F32)
            in_order = h_words.get((s, q, j))
            for first_pass in range(0, PASSES, PAIR_PASSES):
                flipped = flip_pool.tile([P, PAIR_PASSES * 2, P], F32, tag="flip")
                for i in range(PAIR_PASSES):
                    first = (first_pass + i) * (K_PASS // 2)
                    for u in range(2):
                        if in_order is None:
                            pick = words[:, first + u : first + K_PASS // 2 : 2]
                        else:
                            pick = in_order[:, first + P * u : first + P * (u + 1)]
                        nc.tensor.transpose(flipped[:, 2 * i + u, :], pick, ident_f32[:])
                nc.scalar.copy(
                    out=pairs[:, j, first_pass : first_pass + PAIR_PASSES],
                    in_=flipped[:].rearrange("p (i u) r -> p i r u", u=2),
                )

        def order_words(s, q, j):
            in_order = stage.tile([P, F // 2], F32, tag="in_order", bufs=TILES)
            h_words[(s, q, j)] = in_order
            nc.vector.tensor_copy(
                out=in_order[:].rearrange("p (g u n) -> p g u n", g=PASSES, u=2),
                in_=h_raw[(s, TILES * q + j)][:].bitcast(F32).rearrange("p (g n u) -> p g u n", g=PASSES, u=2),
            )

        def flip_hidden(s, q):
            for j in range(TILES):
                flip_tile(s, q, j)

        def quantise_hidden(s, q):
            codes = stage.tile([P, PASSES * COLS], U32, align_bytes=64, tag="h_codes")
            scales = stage.tile([P, PASSES * COLS], U8, align_bytes=64, tag="h_scales")
            nc.vector.quantize_mx(out=codes[:].bitcast(FP8X4), scales=scales[:], in_=h_grouped[(s, q)][:])
            h_codes[(s, q)] = codes
            h_scales[(s, q)] = scales

        def multiply(acc, s, q, m, g, first_tile, tiles):
            rows = slice(P * m, P * (m + 1))
            cols = slice(COLS * g + P * first_tile, COLS * g + P * (first_tile + tiles))
            nc.tensor.matmul_mx(
                out=acc[:],
                lhsT=w_codes[s][:, g, rows].bitcast(FP8X4),
                lhsT_scale=w_scales[s][:, g, rows],
                rhs=h_codes[(s, q)][:, cols].bitcast(FP8X4),
                rhs_scale=h_scales[(s, q)][:, cols],
                start=(g == 0),
                stop=(g == PASSES - 1),
            )

        def add_first_bias(acc, s, q, m, first_tile, tiles):
            if m == 0:
                plain = stage.tile([P, D_TILES * COLS], BF16, tag="cat_plain")
                cat_plain[(s, q, first_tile)] = plain
            width = P * tiles
            nc.scalar.activation(
                out=cat_plain[(s, q, first_tile)][:, width * m : width * (m + 1)],
                in_=acc[:],
                func=ACT.Identity,
                bias=bias_raw[s][:, m : m + 1],
                scale=1.0,
            )

        def first_stage(s, q, first_tile, tiles, fillers):
            for m in range(D_TILES):
                acc = acc_pool.tile([P, P * tiles], F32, tag="acc")
                for g in range(PASSES):
                    multiply(acc, s, q, m, g, first_tile, tiles)
                add_first_bias(acc, s, q, m, first_tile, tiles)
                for filler in fillers[m : m + 1]:
                    filler()

        def regroup_cat(s, q, first_tile, tiles):
            size = PACK * P * tiles
            grouped = stage.tile([P, PACK * COLS], BF16, align_bytes=64, tag="cat_grouped")
            regroup(nc.vector.tensor_copy, grouped[:, 0:size], cat_plain[(s, q, first_tile)][:, 0:size], 0, P * tiles)
            cat_grouped[(s, q, first_tile)] = grouped

        def quantise_cat(s, q, first_tile, tiles):
            codes = keep.tile([P, P * tiles], U32, align_bytes=64, name="cat_codes_%d_%d_%d" % (s, q, first_tile))
            scales = keep.tile([P, P * tiles], U8, align_bytes=64, name="cat_scales_%d_%d_%d" % (s, q, first_tile))
            nc.vector.quantize_mx(
                out=codes[:].bitcast(FP8X4),
                scales=scales[:],
                in_=cat_grouped[(s, q, first_tile)][:, 0 : PACK * P * tiles],
            )
            for j in range(tiles):
                cat_codes[(s, q, first_tile + j)] = codes[:, P * j : P * (j + 1)]
                cat_scales[(s, q, first_tile + j)] = scales[:, P * j : P * (j + 1)]

        def second_stage(q, j):
            y = acc_pool.tile([P, D], F32, tag="acc")
            for s in range(STREAMS):
                nc.tensor.matmul_mx(
                    out=y[:],
                    lhsT=cat_codes[(s, q, j)].bitcast(FP8X4),
                    lhsT_scale=cat_scales[(s, q, j)],
                    rhs=w_codes[2][:, s, :].bitcast(FP8X4),
                    rhs_scale=w_scales[2][:, s, :],
                    start=(s == 0),
                    stop=(s == STREAMS - 1),
                )
            y_banks[(q, j)] = y

        def add_second_bias(q, j):
            wave = tail.tile([P, D], F32, tag="wave", bufs=3 * TILES)
            nc.vector.tensor_tensor(out=wave[:], in0=y_banks[(q, j)][:], in1=be_all[:], op=ALU.add)
            waves[(q, j)] = wave

        def sum_squares(q, j):
            if j == 0:
                total = tail.tile([P, TILES], F32, tag="total")
                totals[q] = total
            squares = tail.tile([P, D], BF16, tag="squares", bufs=2)
            nc.scalar.activation(
                out=squares[:], in_=waves[(q, j)][:], func=ACT.Square, accum_out=totals[q][:, j : j + 1]
            )

        def invert_rms(q, first_tile, tiles):
            if first_tile == 0:
                inv = tail.tile([P, TILES], F32, tag="inv")
                inverses[q] = inv
            cols = slice(first_tile, first_tile + tiles)
            nc.scalar.activation(
                out=inverses[q][:, cols],
                in_=totals[q][:, cols],
                func=ACT.Abs_reciprocal_sqrt,
                bias=eps[:],
                scale=1.0 / D,
            )

        out_view = out.flatten_outer_dims().rearrange("(j p) d -> j p d", p=P)

        def normalise_tile(q, j, pieces=1):
            for i in range(pieces):
                width = D // pieces
                cols = slice(width * i, width * (i + 1))
                normed = tail.tile([P, width], F32, tag="normed", bufs=TOKEN_TILES)
                nc.vector.scalar_tensor_tensor(
                    out=normed[:],
                    in0=waves[(q, j)][:, cols],
                    scalar=inverses[q][:, j : j + 1],
                    in1=g_all[:, cols],
                    op0=ALU.mult,
                    op1=ALU.mult,
                )
                nc.sync.dma_start(out=out_view[TILES * q + j][:, cols], in_=normed[:])

        def unit_at(i):
            return [units[i]] if 0 <= i < len(units) else []

        def quarter_at(i):
            return [q for s, q in unit_at(i) if s == STREAMS - 1]

        first = units[0]
        second = units[1]
        flip_tile(*first, 0)
        flip_tile(*first, 1)
        regroup_chunk(0, 0)
        quantise_chunk(0, 0)
        regroup_chunk(0, 1)
        regroup_chunk(0, 2, nc.scalar.copy)
        quantise_hidden(*first)
        quantise_chunk(0, 1)
        flip_tile(*second, 0)
        sums = []
        for m in range(D_TILES):
            acc = acc_pool.tile([P, COLS], F32, tag="acc")
            sums.append(acc)
        for g in range(PASSES):
            if g == 2:
                regroup_chunk(0, 3)
                quantise_chunk(0, 2)
                quantise_chunk(0, 3)
            for m in range(D_TILES):
                multiply(sums[m], *first, m, g, 0, TILES)
            if g == 1:
                flip_tile(*second, 1)
        for m in range(D_TILES):
            add_first_bias(sums[m], *first, m, 0, TILES)

        def each_tile(work, q):
            for j in range(TILES):
                work(q, j)

        def norms_of(q):
            return [
                lambda: None,
                lambda: sum_squares(q, 0),
                lambda: sum_squares(q, 1),
                lambda: invert_rms(q, 0, TILES),
            ]

        def by_scalar(chunk, first, last, pieces):
            step = (last - first) // pieces
            return [lambda c=c: regroup_chunk(*chunk, nc.scalar.copy, c, c + step) for c in range(first, last, step)]

        own = {0: [(1, 0)], 1: [(1, 1)], 2: [(1, 2), (1, 3)], 4: [(2, 0)]}
        shared = {4: [(2, 1)]}
        HALF = D // 2
        quantise_hidden(*second)
        for step in range(0, len(units) - 1):
            s, q = units[step]
            fillers = []
            if step == 5:
                order_words(*units[7], 0)
            if step > 0:
                quantise_hidden(*units[step + 1])
            for chunk in own.get(step, []):
                regroup_chunk(*chunk)
            for chunk in shared.get(step, []):
                fillers = by_scalar(chunk, 0, HALF, D_TILES)
            for done in quarter_at(step - 2):
                fillers = norms_of(done)
            if step > 0:
                first_stage(s, q, 0, TILES, fillers)
            for chunk in shared.get(step, []):
                regroup_chunk(*chunk, nc.vector.tensor_copy, HALF, D)
            for done in quarter_at(step - 1):
                each_tile(second_stage, done)
                add_second_bias(done, 0)
            regroup_cat(s, q, 0, TILES)
            for chunk in own.get(step, []):
                quantise_chunk(*chunk)
            for done in quarter_at(step - 1):
                add_second_bias(done, 1)
            quantise_cat(s, q, 0, TILES)
            for chunk in shared.get(step, []):
                quantise_chunk(*chunk)
            for ahead in unit_at(step + LOOKAHEAD):
                flip_hidden(*ahead)
            for done in quarter_at(step - 2):
                each_tile(normalise_tile, done)
        s, q = units[-1]
        first_stage(s, q, 0, TILES, norms_of(q - 2))
        each_tile(second_stage, q - 1)
        add_second_bias(q - 1, 0)
        regroup_cat(s, q, 0, TILES)
        add_second_bias(q - 1, 1)
        quantise_cat(s, q, 0, TILES)
        each_tile(sum_squares, q - 1)
        invert_rms(q - 1, 0, TILES)
        each_tile(second_stage, q)
        each_tile(normalise_tile, q - 2)
        each_tile(add_second_bias, q)
        for j in range(TILES):
            sum_squares(q, j)
            invert_rms(q, j, 1)
        each_tile(normalise_tile, q - 1)
        normalise_tile(q, 0)
        normalise_tile(q, 1, 2)
